import numpy as np
import ml_dtypes


def mxq(x, axis, fmt="e4m3"):
    dtype, down = {"e4m3": (ml_dtypes.float8_e4m3fn, 7), "e5m2": (ml_dtypes.float8_e5m2, 14)}[fmt]
    v = np.moveaxis(np.asarray(x, np.float32).astype(ml_dtypes.bfloat16).astype(np.float64), axis, -1)
    blocks = v.reshape(v.shape[:-1] + (-1, 32))
    amax = np.abs(blocks).max(-1, keepdims=True)
    byte = np.maximum(np.where(amax > 0, np.frexp(amax)[1] - 1 + 127, 0) - down, 1)
    scale = np.exp2(byte - 127.0)
    codes = (blocks / scale).astype(np.float32).astype(dtype).astype(np.float64)
    return np.moveaxis((codes * scale).reshape(v.shape), -1, axis)


WIDE = False


def mx_kscale(k):
    if not WIDE:
        return np.ones(k)
    levels = np.array([10, -10, 5, -5, 0])
    a = np.random.permutation(np.resize(levels, k // 512 * 4)).reshape(k // 512, 4)
    idx = np.arange(k)
    return np.exp2(a[idx // 512, idx % 128 // 32])


BF16 = ml_dtypes.bfloat16


def bf(x):
    return np.asarray(x, np.float32).astype(BF16)


def f64(x):
    return np.asarray(x).astype(np.float64)


B, N, D1, D2, F1, F2, F3, F4 = 8192, 1, 256, 256, 512, 64, 32, 16
K = D1 + D2
EPS = 1e-5
SLOPE = 0.2


def setup_inputs():
    s = mx_kscale(K)
    g = np.sqrt(EPS)
    return {"input1": bf(np.random.standard_normal((B, N, D1)) * s[:D1]),
            "input2": bf(np.random.standard_normal((B, N, D2)) * s[D1:]),
            "W1": bf(np.random.standard_normal((F1, K)) * 5.0 * g / np.sqrt(K) / s[None, :]),
            "b1": bf(np.random.standard_normal(F1) * 2.5 * g)}


def reference(input1, input2, W1, b1):
    x = np.concatenate([f64(input1), f64(input2)], axis=2)
    h = (mxq(x, 2, "e4m3") @ mxq(f64(W1), 1, "e4m3").T) + f64(b1)
    m = h.mean(axis=-1, keepdims=True)
    v = np.square(h - m).mean(axis=-1, keepdims=True)
    hn = (h - m) * (1.0 / np.sqrt(v + EPS))
    return np.where(hn >= 0, hn, SLOPE * hn)

@@ -1,0 +1,236 @@
+from contextlib import ExitStack
+
+import concourse.mybir as mybir
+from concourse.masks import make_identity
+
+FLOPS = 2 * 8192 * 512 * 512
+
+F32 = mybir.dt.float32
+BF16 = mybir.dt.bfloat16
+U32 = mybir.dt.uint32
+U8 = mybir.dt.uint8
+FP8X4 = mybir.dt.float8_e4m3fn_x4
+ALU = mybir.AluOpType
+ACT = mybir.ActivationFunctionType
+
+P = 128
+ROWS = 8192
+HALF = 256
+K = 512
+F = 512
+TILES = ROWS // P
+GT = 4
+NG = TILES // GT
+EPS = 1e-5
+SLOPE = 0.2
+CHUNKS = [4, 4, 8, 8, 8, 8, 8, 8, 8]
+V_P3 = ()
+
+
+def tile_fcd_pa_t_kernel(tc, input1, input2, W1, b1, out):
+    nc = tc.nc
+    x_views = (
+        input1.rearrange("(p t) o d -> p (t o d)", t=TILES),
+        input2.rearrange("(p t) o d -> p (t o d)", t=TILES),
+    )
+    out_view = out.rearrange("(p t) o f -> p (t o f)", t=TILES)
+    w_view = W1.rearrange("(j p) k -> p j k", p=P)
+
+    with ExitStack() as stack:
+        const = stack.enter_context(tc.tile_pool(name="const", bufs=1))
+        work = stack.enter_context(tc.tile_pool(name="work", bufs=2))
+        stats = stack.enter_context(tc.tile_pool(name="stats", bufs=6))
+        psum = stack.enter_context(tc.psum_pool(name="psum", bufs=4))
+        stack.enter_context(tc.manual_schedule())
+
+        wraw = const.tile([P, 4 * K], BF16)
+        nc.sync.dma_start(out=wraw[:].rearrange("p (j k) -> p j k", j=4), in_=w_view)
+        braw = const.tile([P, F], BF16)
+        nc.scalar.dma_start(out=braw[:], in_=b1.partition_broadcast(P))
+        x_words = {}
+        first = 0
+        for c, n in enumerate(CHUNKS):
+            views = []
+            for s in range(2):
+                xin = const.tile([P, n * HALF], BF16, name="x%d_%d" % (s, c))
+                nc.sync.dma_start(out=xin[:], in_=x_views[s][:, first * HALF : (first + n) * HALF])
+                views.append(xin[:].bitcast(F32))
+            for t in range(n):
+                x_words[first + t] = (views[0], views[1], t)
+            first += n
+
+        ident = const.tile([P, P], F32)
+        make_identity(nc, ident[:])
+        eps = const.tile([P, 1], F32)
+        nc.vector.memset(eps[:], EPS)
+        warm = const.tile([P, 1], F32)
+        nc.scalar.activation(out=warm[:], in_=eps[:], func=ACT.Sqrt)
+
+        def transpose_group(word_block):
+            banks = []
+            for b in range(2):
+                xt = psum.tile([P, 2, 2, P], F32, tag="xt")
+                for jj in range(2):
+                    for u in range(2):
+                        nc.tensor.transpose(xt[:, jj, u, :], word_block(2 * b + jj, u), ident[:])
+                banks.append(xt)
+            return banks
+
+        def regroup(banks, tag):
+            grouped = work.tile([P, GT * K], BF16, tag=tag, align_bytes=64)
+            gw = grouped[:].bitcast(F32).rearrange("p (j r u) -> p j r u", j=GT, u=2)
+            for b in range(2):
+                nc.scalar.copy(
+                    out=gw[:, 2 * b : 2 * b + 2, :, :],
+                    in_=banks[b][:].rearrange("p j u r -> p j r u"),
+                )
+            return grouped
+
+        def quantise(grouped, tag):
+            codes = work.tile([P, GT * P], U32, tag=tag + "c", align_bytes=64)
+            scales = work.tile([P, GT * P], U8, tag=tag + "s", align_bytes=64)
+            nc.vector.quantize_mx(out=codes[:].bitcast(FP8X4), scales=scales[:], in_=grouped[:])
+            return codes, scales
+
+        wf = wraw[:].bitcast(F32)
+        w_banks = transpose_group(lambda j, u: wf[:, j * HALF + u * P : j * HALF + (u + 1) * P])
+        w_grouped = regroup(w_banks, "wg")
+        w_codes, w_scales = quantise(w_grouped, "w")
+        bias = const.tile([P, F], F32)
+        nc.vector.tensor_copy(out=bias[:], in_=braw[:])
+
+        live = {}
+
+        def x_block(g):
+            def block(j, u):
+                entry = x_words[g * GT + j]
+                return entry[u][:, entry[2] * P : (entry[2] + 1) * P]
+
+            return block
+
+        def stage_transpose(g):
+            live[("banks", g)] = transpose_group(x_block(g))
+
+        def stage_regroup(g):
+            live[("grouped", g)] = regroup(live[("banks", g)], "xg")
+
+        def stage_quantise(g):
+            live[("q", g)] = quantise(live[("grouped", g)], "x")
+
+        def stage_matmul(g):
+            codes, scales = live[("q", g)]
+            ys = []
+            for j in range(GT):
+                y = psum.tile([P, F], F32, tag="y")
+                nc.tensor.matmul_mx(
+                    out=y[:],
+                    lhsT=codes[:, j * P : (j + 1) * P].bitcast(FP8X4),
+                    lhsT_scale=scales[:, j * P : (j + 1) * P],
+                    rhs=w_codes[:].bitcast(FP8X4),
+                    rhs_scale=w_scales[:],
+                    start=True,
+                    stop=True,
+                )
+                ys.append(y)
+            live[("y", g)] = ys
+
+        def stage_bias(g):
+            ys = live[("y", g)]
+            h = work.tile([P, GT, F], F32, tag="h", bufs=4)
+            sums = stats.tile([P, GT], F32, tag="sums")
+            for j in range(GT):
+                nc.vector.scalar_tensor_tensor(
+                    out=h[:, j, :],
+                    in0=ys[j][:],
+                    scalar=1.0,
+                    in1=bias[:],
+                    op0=ALU.mult,
+                    op1=ALU.add,
+                    accum_out=sums[:, j : j + 1],
+                )
+            negm = stats.tile([P, GT], F32, tag="negm")
+            nc.vector.tensor_scalar_mul(out=negm[:], in0=sums[:], scalar1=-1.0 / F)
+            live[("h", g)] = (h, negm)
+
+        def stage_squares(g):
+            h, negm = live[("h", g)]
+            ssq = stats.tile([P, GT], F32, tag="ssq")
+            for j in range(GT):
+                junk = work.tile([P, F], BF16, tag="junk")
+                nc.scalar.activation(
+                    out=junk[:],
+                    in_=h[:, j, :],
+                    func=ACT.Square,
+                    bias=negm[:, j : j + 1],
+                    scale=1.0,
+                    accum_out=ssq[:, j : j + 1],
+                )
+            std = stats.tile([P, GT], F32, tag="std")
+            nc.scalar.activation(out=std[:], in_=ssq[:], func=ACT.Sqrt, bias=eps[:], scale=1.0 / F)
+            live[("std", g)] = std
+
+        def stage_rstd(g):
+            std = live[("std", g)]
+            negm = live[("h", g)][1]
+            rstd = stats.tile([P, GT], F32, tag="rstd")
+            nc.vector.reciprocal(out=rstd[:], in_=std[:])
+            shift = stats.tile([P, GT], F32, tag="shift")
+            nc.vector.tensor_mul(out=shift[:], in0=negm[:], in1=rstd[:])
+            live[("r", g)] = (rstd, shift)
+
+        def stage_norm(g, engine):
+            h = live[("h", g)][0]
+            rstd, shift = live[("r", g)]
+            if ("z", g) not in live:
+                z_new = work.tile([P, GT, F], F32, tag="z", bufs=3)
+                live[("z", g)] = z_new
+            z = live[("z", g)]
+            for j in range(GT):
+                if engine == "scalar" and j not in V_P3:
+                    nc.scalar.activation(
+                        out=z[:, j, :],
+                        in_=h[:, j, :],
+                        func=ACT.Identity,
+                        bias=shift[:, j : j + 1],
+                        scale=rstd[:, j : j + 1],
+                    )
+                if engine == "vector" and j in V_P3:
+                    nc.vector.tensor_scalar(
+                        out=z[:, j, :],
+                        in0=h[:, j, :],
+                        scalar1=rstd[:, j : j + 1],
+                        scalar2=shift[:, j : j + 1],
+                        op0=ALU.mult,
+                        op1=ALU.add,
+                    )
+
+        def stage_leaky(g):
+            z = live[("z", g)]
+            o = work.tile([P, GT * F], F32, tag="o", bufs=3)
+            zf = z[:].rearrange("p j f -> p (j f)")
+            nc.vector.scalar_tensor_tensor(
+                out=o[:], in0=zf, scalar=SLOPE, in1=zf, op0=ALU.mult, op1=ALU.max
+            )
+            nc.sync.dma_start(out=out_view[:, g * GT * F : (g + 1) * GT * F], in_=o[:])
+
+        def on(g):
+            return 0 <= g < NG
+
+        for i in range(NG + 4):
+            if on(i):
+                stage_transpose(i)
+                stage_regroup(i)
+            if on(i - 1):
+                stage_quantise(i - 1)
+                stage_matmul(i - 1)
+            if on(i - 4):
+                stage_leaky(i - 4)
+            if on(i - 2):
+                stage_squares(i - 2)
+            if on(i - 3):
+                stage_norm(i - 3, "vector")
+                stage_norm(i - 3, "scalar")
+            if on(i - 1):
+                stage_bias(i - 1)
+            if on(i - 2):
+                stage_rstd(i - 2)

@@ -24,7 +24,7 @@ NG = TILES // GT
 EPS = 1e-5
 SLOPE = 0.2
 CHUNKS = [4, 4, 8, 8, 8, 8, 8, 8, 8]
-V_P3 = ()
+VECTOR_NORM_TILES = 1
 
 
 def tile_fcd_pa_t_kernel(tc, input1, input2, W1, b1, out):
@@ -39,7 +39,7 @@ def tile_fcd_pa_t_kernel(tc, input1, input2, W1, b1, out):
     with ExitStack() as stack:
         const = stack.enter_context(tc.tile_pool(name="const", bufs=1))
         work = stack.enter_context(tc.tile_pool(name="work", bufs=2))
-        stats = stack.enter_context(tc.tile_pool(name="stats", bufs=6))
+        stats = stack.enter_context(tc.tile_pool(name="stats", bufs=8))
         psum = stack.enter_context(tc.psum_pool(name="psum", bufs=4))
         stack.enter_context(tc.manual_schedule())
 
@@ -61,10 +61,10 @@ def tile_fcd_pa_t_kernel(tc, input1, input2, W1, b1, out):
 
         ident = const.tile([P, P], F32)
         make_identity(nc, ident[:])
-        eps = const.tile([P, 1], F32)
-        nc.vector.memset(eps[:], EPS)
+        one = const.tile([P, 1], F32)
+        nc.vector.memset(one[:], 1.0)
         warm = const.tile([P, 1], F32)
-        nc.scalar.activation(out=warm[:], in_=eps[:], func=ACT.Sqrt)
+        nc.scalar.activation(out=warm[:], in_=one[:], func=ACT.Sqrt)
 
         def transpose_group(word_block):
             banks = []
@@ -76,26 +76,23 @@ def tile_fcd_pa_t_kernel(tc, input1, input2, W1, b1, out):
                 banks.append(xt)
             return banks
 
-        def regroup(banks, tag):
-            grouped = work.tile([P, GT * K], BF16, tag=tag, align_bytes=64)
+        def regroup(banks, grouped, on_vector):
             gw = grouped[:].bitcast(F32).rearrange("p (j r u) -> p j r u", j=GT, u=2)
             for b in range(2):
-                nc.scalar.copy(
-                    out=gw[:, 2 * b : 2 * b + 2, :, :],
-                    in_=banks[b][:].rearrange("p j u r -> p j r u"),
-                )
-            return grouped
-
-        def quantise(grouped, tag):
-            codes = work.tile([P, GT * P], U32, tag=tag + "c", align_bytes=64)
-            scales = work.tile([P, GT * P], U8, tag=tag + "s", align_bytes=64)
-            nc.vector.quantize_mx(out=codes[:].bitcast(FP8X4), scales=scales[:], in_=grouped[:])
-            return codes, scales
+                dst = gw[:, 2 * b : 2 * b + 2, :, :]
+                src = banks[b][:].rearrange("p j u r -> p j r u")
+                if on_vector:
+                    nc.vector.tensor_copy(out=dst, in_=src)
+                else:
+                    nc.scalar.copy(out=dst, in_=src)
 
         wf = wraw[:].bitcast(F32)
         w_banks = transpose_group(lambda j, u: wf[:, j * HALF + u * P : j * HALF + (u + 1) * P])
-        w_grouped = regroup(w_banks, "wg")
-        w_codes, w_scales = quantise(w_grouped, "w")
+        w_grouped = const.tile([P, GT * K], BF16, align_bytes=64)
+        regroup(w_banks, w_grouped, True)
+        w_codes = const.tile([P, F], U32, align_bytes=64)
+        w_scales = const.tile([P, F], U8, align_bytes=64)
+        nc.vector.quantize_mx(out=w_codes[:].bitcast(FP8X4), scales=w_scales[:], in_=w_grouped[:])
         bias = const.tile([P, F], F32)
         nc.vector.tensor_copy(out=bias[:], in_=braw[:])
 
@@ -109,16 +106,17 @@ def tile_fcd_pa_t_kernel(tc, input1, input2, W1, b1, out):
             return block
 
         def stage_transpose(g):
-            live[("banks", g)] = transpose_group(x_block(g))
-
-        def stage_regroup(g):
-            live[("grouped", g)] = regroup(live[("banks", g)], "xg")
-
-        def stage_quantise(g):
-            live[("q", g)] = quantise(live[("grouped", g)], "x")
+            banks = transpose_group(x_block(g))
+            grouped = work.tile([P, GT * K], BF16, tag="xg", align_bytes=64)
+            regroup(banks, grouped, False)
+            live[("grouped", g)] = grouped
 
         def stage_matmul(g):
-            codes, scales = live[("q", g)]
+            codes = work.tile([P, GT * P], U32, tag="xc", align_bytes=64)
+            scales = work.tile([P, GT * P], U8, tag="xs", align_bytes=64)
+            nc.vector.quantize_mx(
+                out=codes[:].bitcast(FP8X4), scales=scales[:], in_=live[("grouped", g)][:]
+            )
             ys = []
             for j in range(GT):
                 y = psum.tile([P, F], F32, tag="y")
@@ -136,7 +134,7 @@ def tile_fcd_pa_t_kernel(tc, input1, input2, W1, b1, out):
 
         def stage_bias(g):
             ys = live[("y", g)]
-            h = work.tile([P, GT, F], F32, tag="h", bufs=4)
+            h = work.tile([P, GT, F], F32, tag="h", bufs=5)
             sums = stats.tile([P, GT], F32, tag="sums")
             for j in range(GT):
                 nc.vector.scalar_tensor_tensor(
@@ -166,7 +164,7 @@ def tile_fcd_pa_t_kernel(tc, input1, input2, W1, b1, out):
                     accum_out=ssq[:, j : j + 1],
                 )
             std = stats.tile([P, GT], F32, tag="std")
-            nc.scalar.activation(out=std[:], in_=ssq[:], func=ACT.Sqrt, bias=eps[:], scale=1.0 / F)
+            nc.scalar.activation(out=std[:], in_=ssq[:], func=ACT.Sqrt, bias=EPS, scale=1.0 / F)
             live[("std", g)] = std
 
         def stage_rstd(g):
@@ -178,59 +176,67 @@ def tile_fcd_pa_t_kernel(tc, input1, input2, W1, b1, out):
             nc.vector.tensor_mul(out=shift[:], in0=negm[:], in1=rstd[:])
             live[("r", g)] = (rstd, shift)
 
-        def stage_norm(g, engine):
+        def norm_tile(g, z, j):
             h = live[("h", g)][0]
             rstd, shift = live[("r", g)]
-            if ("z", g) not in live:
-                z_new = work.tile([P, GT, F], F32, tag="z", bufs=3)
-                live[("z", g)] = z_new
-            z = live[("z", g)]
-            for j in range(GT):
-                if engine == "scalar" and j not in V_P3:
-                    nc.scalar.activation(
-                        out=z[:, j, :],
-                        in_=h[:, j, :],
-                        func=ACT.Identity,
-                        bias=shift[:, j : j + 1],
-                        scale=rstd[:, j : j + 1],
-                    )
-                if engine == "vector" and j in V_P3:
-                    nc.vector.tensor_scalar(
-                        out=z[:, j, :],
-                        in0=h[:, j, :],
-                        scalar1=rstd[:, j : j + 1],
-                        scalar2=shift[:, j : j + 1],
-                        op0=ALU.mult,
-                        op1=ALU.add,
-                    )
+            if j < VECTOR_NORM_TILES:
+                nc.vector.tensor_scalar(
+                    out=z[:, j, :],
+                    in0=h[:, j, :],
+                    scalar1=rstd[:, j : j + 1],
+                    scalar2=shift[:, j : j + 1],
+                    op0=ALU.mult,
+                    op1=ALU.add,
+                )
+            else:
+                nc.scalar.activation(
+                    out=z[:, j, :],
+                    in_=h[:, j, :],
+                    func=ACT.Identity,
+                    bias=shift[:, j : j + 1],
+                    scale=rstd[:, j : j + 1],
+                )
+
+        def leaky_store(g, z, o, j0, j1):
+            zf = z[:, j0:j1, :].rearrange("p j f -> p (j f)")
+            nc.vector.scalar_tensor_tensor(
+                out=o[:, j0 * F : j1 * F], in0=zf, scalar=SLOPE, in1=zf, op0=ALU.mult, op1=ALU.max
+            )
+            nc.sync.dma_start(
+                out=out_view[:, (g * GT + j0) * F : (g * GT + j1) * F], in_=o[:, j0 * F : j1 * F]
+            )
+
+        def stage_norm(g):
+            z = work.tile([P, GT, F], F32, tag="z", bufs=3)
+            live[("z", g)] = z
+            if g < NG - 1:
+                for j in range(GT):
+                    norm_tile(g, z, j)
+            else:
+                o = work.tile([P, GT * F], F32, tag="o", bufs=3)
+                for j in range(GT):
+                    norm_tile(g, z, j)
+                    leaky_store(g, z, o, j, j + 1)
 
         def stage_leaky(g):
-            z = live[("z", g)]
             o = work.tile([P, GT * F], F32, tag="o", bufs=3)
-            zf = z[:].rearrange("p j f -> p (j f)")
-            nc.vector.scalar_tensor_tensor(
-                out=o[:], in0=zf, scalar=SLOPE, in1=zf, op0=ALU.mult, op1=ALU.max
-            )
-            nc.sync.dma_start(out=out_view[:, g * GT * F : (g + 1) * GT * F], in_=o[:])
+            leaky_store(g, live[("z", g)], o, 0, GT)
 
         def on(g):
             return 0 <= g < NG
 
-        for i in range(NG + 4):
+        for i in range(NG + 5):
             if on(i):
                 stage_transpose(i)
-                stage_regroup(i)
             if on(i - 1):
-                stage_quantise(i - 1)
                 stage_matmul(i - 1)
+            if on(i - 5) and i - 5 < NG - 1:
+                stage_leaky(i - 5)
+            if on(i - 3):
+                stage_rstd(i - 3)
             if on(i - 4):
-                stage_leaky(i - 4)
+                stage_norm(i - 4)
             if on(i - 2):
                 stage_squares(i - 2)
-            if on(i - 3):
-                stage_norm(i - 3, "vector")
-                stage_norm(i - 3, "scalar")
             if on(i - 1):
                 stage_bias(i - 1)
-            if on(i - 2):
-                stage_rstd(i - 2)

@@ -76,20 +76,20 @@ def tile_fcd_pa_t_kernel(tc, input1, input2, W1, b1, out):
                 banks.append(xt)
             return banks
 
-        def regroup(banks, grouped, on_vector):
+        def regroup(banks, grouped, b, on_vector):
             gw = grouped[:].bitcast(F32).rearrange("p (j r u) -> p j r u", j=GT, u=2)
-            for b in range(2):
-                dst = gw[:, 2 * b : 2 * b + 2, :, :]
-                src = banks[b][:].rearrange("p j u r -> p j r u")
-                if on_vector:
-                    nc.vector.tensor_copy(out=dst, in_=src)
-                else:
-                    nc.scalar.copy(out=dst, in_=src)
+            dst = gw[:, 2 * b : 2 * b + 2, :, :]
+            src = banks[b][:].rearrange("p j u r -> p j r u")
+            if on_vector:
+                nc.vector.tensor_copy(out=dst, in_=src)
+            else:
+                nc.scalar.copy(out=dst, in_=src)
 
         wf = wraw[:].bitcast(F32)
         w_banks = transpose_group(lambda j, u: wf[:, j * HALF + u * P : j * HALF + (u + 1) * P])
         w_grouped = const.tile([P, GT * K], BF16, align_bytes=64)
-        regroup(w_banks, w_grouped, True)
+        regroup(w_banks, w_grouped, 0, True)
+        regroup(w_banks, w_grouped, 1, True)
         w_codes = const.tile([P, F], U32, align_bytes=64)
         w_scales = const.tile([P, F], U8, align_bytes=64)
         nc.vector.quantize_mx(out=w_codes[:].bitcast(FP8X4), scales=w_scales[:], in_=w_grouped[:])
@@ -97,6 +97,9 @@ def tile_fcd_pa_t_kernel(tc, input1, input2, W1, b1, out):
         nc.vector.tensor_copy(out=bias[:], in_=braw[:])
 
         live = {}
+
+        def on(g):
+            return 0 <= g < NG
 
         def x_block(g):
             def block(j, u):
@@ -108,7 +111,10 @@ def tile_fcd_pa_t_kernel(tc, input1, input2, W1, b1, out):
         def stage_transpose(g):
             banks = transpose_group(x_block(g))
             grouped = work.tile([P, GT * K], BF16, tag="xg", align_bytes=64)
-            regroup(banks, grouped, False)
+            regroup(banks, grouped, 0, False)
+            if on(g - 3):
+                stage_std(g - 3)
+            regroup(banks, grouped, 1, False)
             live[("grouped", g)] = grouped
 
         def stage_matmul(g):
@@ -146,12 +152,19 @@ def tile_fcd_pa_t_kernel(tc, input1, input2, W1, b1, out):
                     op1=ALU.add,
                     accum_out=sums[:, j : j + 1],
                 )
+                if j == 0 and on(g - 2):
+                    stage_shift(g - 2)
+            live[("h", g)] = h
+            live[("sums", g)] = sums
+
+        def stage_negm(g):
             negm = stats.tile([P, GT], F32, tag="negm")
-            nc.vector.tensor_scalar_mul(out=negm[:], in0=sums[:], scalar1=-1.0 / F)
-            live[("h", g)] = (h, negm)
+            nc.vector.tensor_scalar_mul(out=negm[:], in0=live[("sums", g)][:], scalar1=-1.0 / F)
+            live[("negm", g)] = negm
 
         def stage_squares(g):
-            h, negm = live[("h", g)]
+            h = live[("h", g)]
+            negm = live[("negm", g)]
             ssq = stats.tile([P, GT], F32, tag="ssq")
             for j in range(GT):
                 junk = work.tile([P, F], BF16, tag="junk")
@@ -163,22 +176,29 @@ def tile_fcd_pa_t_kernel(tc, input1, input2, W1, b1, out):
                     scale=1.0,
                     accum_out=ssq[:, j : j + 1],
                 )
+            live[("ssq", g)] = ssq
+
+        def stage_std(g):
             std = stats.tile([P, GT], F32, tag="std")
-            nc.scalar.activation(out=std[:], in_=ssq[:], func=ACT.Sqrt, bias=EPS, scale=1.0 / F)
+            nc.scalar.activation(
+                out=std[:], in_=live[("ssq", g)][:], func=ACT.Sqrt, bias=EPS, scale=1.0 / F
+            )
             live[("std", g)] = std
 
         def stage_rstd(g):
-            std = live[("std", g)]
-            negm = live[("h", g)][1]
             rstd = stats.tile([P, GT], F32, tag="rstd")
-            nc.vector.reciprocal(out=rstd[:], in_=std[:])
+            nc.vector.reciprocal(out=rstd[:], in_=live[("std", g)][:])
+            live[("rstd", g)] = rstd
+
+        def stage_shift(g):
             shift = stats.tile([P, GT], F32, tag="shift")
-            nc.vector.tensor_mul(out=shift[:], in0=negm[:], in1=rstd[:])
-            live[("r", g)] = (rstd, shift)
+            nc.vector.tensor_mul(out=shift[:], in0=live[("negm", g)][:], in1=live[("rstd", g)][:])
+            live[("shift", g)] = shift
 
         def norm_tile(g, z, j):
-            h = live[("h", g)][0]
-            rstd, shift = live[("r", g)]
+            h = live[("h", g)]
+            rstd = live[("rstd", g)]
+            shift = live[("shift", g)]
             if j < VECTOR_NORM_TILES:
                 nc.vector.tensor_scalar(
                     out=z[:, j, :],
@@ -209,34 +229,37 @@ def tile_fcd_pa_t_kernel(tc, input1, input2, W1, b1, out):
         def stage_norm(g):
             z = work.tile([P, GT, F], F32, tag="z", bufs=3)
             live[("z", g)] = z
-            if g < NG - 1:
-                for j in range(GT):
-                    norm_tile(g, z, j)
-            else:
-                o = work.tile([P, GT * F], F32, tag="o", bufs=3)
-                for j in range(GT):
-                    norm_tile(g, z, j)
-                    leaky_store(g, z, o, j, j + 1)
+            for j in range(GT):
+                norm_tile(g, z, j)
 
         def stage_leaky(g):
             o = work.tile([P, GT * F], F32, tag="o", bufs=3)
-            leaky_store(g, live[("z", g)], o, 0, GT)
-
-        def on(g):
-            return 0 <= g < NG
+            if g < NG - 1:
+                leaky_store(g, live[("z", g)], o, 0, GT)
+            else:
+                for j in range(GT):
+                    leaky_store(g, live[("z", g)], o, j, j + 1)
 
         for i in range(NG + 5):
             if on(i):
                 stage_transpose(i)
+            elif on(i - 3):
+                stage_std(i - 3)
             if on(i - 1):
                 stage_matmul(i - 1)
-            if on(i - 5) and i - 5 < NG - 1:
-                stage_leaky(i - 5)
-            if on(i - 3):
-                stage_rstd(i - 3)
+            if on(i - 2):
+                stage_negm(i - 2)
             if on(i - 4):
                 stage_norm(i - 4)
+            if on(i - 5) and i - 5 < NG - 1:
+                stage_leaky(i - 5)
+            if i - 4 == NG - 1:
+                stage_leaky(i - 4)
+            if on(i - 3):
+                stage_rstd(i - 3)
             if on(i - 2):
                 stage_squares(i - 2)
             if on(i - 1):
                 stage_bias(i - 1)
+            elif on(i - 3):
+                stage_shift(i - 3)

@@ -24,7 +24,7 @@ NG = TILES // GT
 EPS = 1e-5
 SLOPE = 0.2
 CHUNKS = [4, 4, 8, 8, 8, 8, 8, 8, 8]
-VECTOR_NORM_TILES = 1
+GPSIMD_NORM_TILES = 1
 
 
 def tile_fcd_pa_t_kernel(tc, input1, input2, W1, b1, out):
@@ -152,19 +152,12 @@ def tile_fcd_pa_t_kernel(tc, input1, input2, W1, b1, out):
                     op1=ALU.add,
                     accum_out=sums[:, j : j + 1],
                 )
-                if j == 0 and on(g - 2):
-                    stage_shift(g - 2)
             live[("h", g)] = h
             live[("sums", g)] = sums
 
-        def stage_negm(g):
-            negm = stats.tile([P, GT], F32, tag="negm")
-            nc.vector.tensor_scalar_mul(out=negm[:], in0=live[("sums", g)][:], scalar1=-1.0 / F)
-            live[("negm", g)] = negm
-
         def stage_squares(g):
             h = live[("h", g)]
-            negm = live[("negm", g)]
+            sums = live[("sums", g)]
             ssq = stats.tile([P, GT], F32, tag="ssq")
             for j in range(GT):
                 junk = work.tile([P, F], BF16, tag="junk")
@@ -172,8 +165,8 @@ def tile_fcd_pa_t_kernel(tc, input1, input2, W1, b1, out):
                     out=junk[:],
                     in_=h[:, j, :],
                     func=ACT.Square,
-                    bias=negm[:, j : j + 1],
-                    scale=1.0,
+                    bias=sums[:, j : j + 1],
+                    scale=-1.0 * F,
                     accum_out=ssq[:, j : j + 1],
                 )
             live[("ssq", g)] = ssq
@@ -181,7 +174,11 @@ def tile_fcd_pa_t_kernel(tc, input1, input2, W1, b1, out):
         def stage_std(g):
             std = stats.tile([P, GT], F32, tag="std")
             nc.scalar.activation(
-                out=std[:], in_=live[("ssq", g)][:], func=ACT.Sqrt, bias=EPS, scale=1.0 / F
+                out=std[:],
+                in_=live[("ssq", g)][:],
+                func=ACT.Sqrt,
+                bias=EPS,
+                scale=1.0 / (F * F * F),
             )
             live[("std", g)] = std
 
@@ -192,15 +189,22 @@ def tile_fcd_pa_t_kernel(tc, input1, input2, W1, b1, out):
 
         def stage_shift(g):
             shift = stats.tile([P, GT], F32, tag="shift")
-            nc.vector.tensor_mul(out=shift[:], in0=live[("negm", g)][:], in1=live[("rstd", g)][:])
+            nc.vector.scalar_tensor_tensor(
+                out=shift[:],
+                in0=live[("sums", g)][:],
+                scalar=-1.0 / F,
+                in1=live[("rstd", g)][:],
+                op0=ALU.mult,
+                op1=ALU.mult,
+            )
             live[("shift", g)] = shift
 
         def norm_tile(g, z, j):
             h = live[("h", g)]
             rstd = live[("rstd", g)]
             shift = live[("shift", g)]
-            if j < VECTOR_NORM_TILES:
-                nc.vector.tensor_scalar(
+            if j < GPSIMD_NORM_TILES:
+                nc.gpsimd.tensor_scalar(
                     out=z[:, j, :],
                     in0=h[:, j, :],
                     scalar1=rstd[:, j : j + 1],
@@ -247,8 +251,8 @@ def tile_fcd_pa_t_kernel(tc, input1, input2, W1, b1, out):
                 stage_std(i - 3)
             if on(i - 1):
                 stage_matmul(i - 1)
-            if on(i - 2):
-                stage_negm(i - 2)
+            if on(i - 3):
+                stage_rstd(i - 3)
             if on(i - 4):
                 stage_norm(i - 4)
             if on(i - 5) and i - 5 < NG - 1:
@@ -256,10 +260,8 @@ def tile_fcd_pa_t_kernel(tc, input1, input2, W1, b1, out):
             if i - 4 == NG - 1:
                 stage_leaky(i - 4)
             if on(i - 3):
-                stage_rstd(i - 3)
+                stage_shift(i - 3)
             if on(i - 2):
                 stage_squares(i - 2)
             if on(i - 1):
                 stage_bias(i - 1)
-            elif on(i - 3):
-                stage_shift(i - 3)

@@ -24,7 +24,7 @@ NG = TILES // GT
 EPS = 1e-5
 SLOPE = 0.2
 CHUNKS = [4, 4, 8, 8, 8, 8, 8, 8, 8]
-GPSIMD_NORM_TILES = 1
+GPSIMD_NORM_TILES = 2
 
 
 def tile_fcd_pa_t_kernel(tc, input1, input2, W1, b1, out):

@@ -43,8 +43,13 @@ def tile_fcd_pa_t_kernel(tc, input1, input2, W1, b1, out):
         psum = stack.enter_context(tc.psum_pool(name="psum", bufs=4))
         stack.enter_context(tc.manual_schedule())
 
-        wraw = const.tile([P, 4 * K], BF16)
-        nc.sync.dma_start(out=wraw[:].rearrange("p (j k) -> p j k", j=4), in_=w_view)
+        w_words = []
+        for b in range(2):
+            wraw = const.tile([P, 2 * K], BF16, name="wraw%d" % b)
+            nc.sync.dma_start(
+                out=wraw[:].rearrange("p (j k) -> p j k", j=2), in_=w_view[:, 2 * b : 2 * b + 2, :]
+            )
+            w_words.append(wraw[:].bitcast(F32))
         braw = const.tile([P, F], BF16)
         nc.scalar.dma_start(out=braw[:], in_=b1.partition_broadcast(P))
         x_words = {}
@@ -64,7 +69,7 @@ def tile_fcd_pa_t_kernel(tc, input1, input2, W1, b1, out):
         one = const.tile([P, 1], F32)
         nc.vector.memset(one[:], 1.0)
         warm = const.tile([P, 1], F32)
-        nc.scalar.activation(out=warm[:], in_=one[:], func=ACT.Sqrt)
+        nc.scalar.activation(out=warm[:], in_=one[:], func=ACT.Abs_reciprocal_sqrt)
 
         def transpose_group(word_block):
             banks = []
@@ -85,8 +90,11 @@ def tile_fcd_pa_t_kernel(tc, input1, input2, W1, b1, out):
             else:
                 nc.scalar.copy(out=dst, in_=src)
 
-        wf = wraw[:].bitcast(F32)
-        w_banks = transpose_group(lambda j, u: wf[:, j * HALF + u * P : j * HALF + (u + 1) * P])
+        def w_block(j, u):
+            start = (j % 2) * HALF + u * P
+            return w_words[j // 2][:, start : start + P]
+
+        w_banks = transpose_group(w_block)
         w_grouped = const.tile([P, GT * K], BF16, align_bytes=64)
         regroup(w_banks, w_grouped, 0, True)
         regroup(w_banks, w_grouped, 1, True)
@@ -109,51 +117,54 @@ def tile_fcd_pa_t_kernel(tc, input1, input2, W1, b1, out):
             return block
 
         def stage_transpose(g):
-            banks = transpose_group(x_block(g))
+            live[("banks", g)] = transpose_group(x_block(g))
+
+        def stage_regroup(g):
+            banks = live[("banks", g)]
             grouped = work.tile([P, GT * K], BF16, tag="xg", align_bytes=64)
             regroup(banks, grouped, 0, False)
-            if on(g - 3):
-                stage_std(g - 3)
+            if on(g - 4):
+                stage_rstd(g - 4)
             regroup(banks, grouped, 1, False)
             live[("grouped", g)] = grouped
 
-        def stage_matmul(g):
+        def stage_quantise(g):
             codes = work.tile([P, GT * P], U32, tag="xc", align_bytes=64)
             scales = work.tile([P, GT * P], U8, tag="xs", align_bytes=64)
             nc.vector.quantize_mx(
                 out=codes[:].bitcast(FP8X4), scales=scales[:], in_=live[("grouped", g)][:]
             )
-            ys = []
-            for j in range(GT):
-                y = psum.tile([P, F], F32, tag="y")
-                nc.tensor.matmul_mx(
-                    out=y[:],
-                    lhsT=codes[:, j * P : (j + 1) * P].bitcast(FP8X4),
-                    lhsT_scale=scales[:, j * P : (j + 1) * P],
-                    rhs=w_codes[:].bitcast(FP8X4),
-                    rhs_scale=w_scales[:],
-                    start=True,
-                    stop=True,
-                )
-                ys.append(y)
-            live[("y", g)] = ys
+            live[("q", g)] = (codes, scales)
 
-        def stage_bias(g):
-            ys = live[("y", g)]
-            h = work.tile([P, GT, F], F32, tag="h", bufs=5)
-            sums = stats.tile([P, GT], F32, tag="sums")
-            for j in range(GT):
-                nc.vector.scalar_tensor_tensor(
-                    out=h[:, j, :],
-                    in0=ys[j][:],
-                    scalar=1.0,
-                    in1=bias[:],
-                    op0=ALU.mult,
-                    op1=ALU.add,
-                    accum_out=sums[:, j : j + 1],
-                )
-            live[("h", g)] = h
-            live[("sums", g)] = sums
+        def matmul_tile(g, j):
+            codes, scales = live[("q", g)]
+            y = psum.tile([P, F], F32, tag="y")
+            nc.tensor.matmul_mx(
+                out=y[:],
+                lhsT=codes[:, j * P : (j + 1) * P].bitcast(FP8X4),
+                lhsT_scale=scales[:, j * P : (j + 1) * P],
+                rhs=w_codes[:].bitcast(FP8X4),
+                rhs_scale=w_scales[:],
+                start=True,
+                stop=True,
+            )
+            live[("y", g, j)] = y
+
+        def bias_tile(g, j):
+            if j == 0:
+                h_new = work.tile([P, GT, F], F32, tag="h", bufs=5)
+                sums_new = stats.tile([P, GT], F32, tag="sums")
+                live[("h", g)] = h_new
+                live[("sums", g)] = sums_new
+            nc.vector.scalar_tensor_tensor(
+                out=live[("h", g)][:, j, :],
+                in0=live[("y", g, j)][:],
+                scalar=1.0,
+                in1=bias[:],
+                op0=ALU.mult,
+                op1=ALU.add,
+                accum_out=live[("sums", g)][:, j : j + 1],
+            )
 
         def stage_squares(g):
             h = live[("h", g)]
@@ -171,20 +182,15 @@ def tile_fcd_pa_t_kernel(tc, input1, input2, W1, b1, out):
                 )
             live[("ssq", g)] = ssq
 
-        def stage_std(g):
-            std = stats.tile([P, GT], F32, tag="std")
+        def stage_rstd(g):
+            rstd = stats.tile([P, GT], F32, tag="rstd")
             nc.scalar.activation(
-                out=std[:],
+                out=rstd[:],
                 in_=live[("ssq", g)][:],
-                func=ACT.Sqrt,
+                func=ACT.Abs_reciprocal_sqrt,
                 bias=EPS,
                 scale=1.0 / (F * F * F),
             )
-            live[("std", g)] = std
-
-        def stage_rstd(g):
-            rstd = stats.tile([P, GT], F32, tag="rstd")
-            nc.vector.reciprocal(out=rstd[:], in_=live[("std", g)][:])
             live[("rstd", g)] = rstd
 
         def stage_shift(g):
@@ -199,27 +205,30 @@ def tile_fcd_pa_t_kernel(tc, input1, input2, W1, b1, out):
             )
             live[("shift", g)] = shift
 
-        def norm_tile(g, z, j):
+        def stage_norm(g):
             h = live[("h", g)]
             rstd = live[("rstd", g)]
             shift = live[("shift", g)]
-            if j < GPSIMD_NORM_TILES:
-                nc.gpsimd.tensor_scalar(
-                    out=z[:, j, :],
-                    in0=h[:, j, :],
-                    scalar1=rstd[:, j : j + 1],
-                    scalar2=shift[:, j : j + 1],
-                    op0=ALU.mult,
-                    op1=ALU.add,
-                )
-            else:
-                nc.scalar.activation(
-                    out=z[:, j, :],
-                    in_=h[:, j, :],
-                    func=ACT.Identity,
-                    bias=shift[:, j : j + 1],
-                    scale=rstd[:, j : j + 1],
-                )
+            z = work.tile([P, GT, F], F32, tag="z", bufs=3)
+            live[("z", g)] = z
+            for j in range(GT):
+                if j < GPSIMD_NORM_TILES and g < NG - 1:
+                    nc.gpsimd.tensor_scalar(
+                        out=z[:, j, :],
+                        in0=h[:, j, :],
+                        scalar1=rstd[:, j : j + 1],
+                        scalar2=shift[:, j : j + 1],
+                        op0=ALU.mult,
+                        op1=ALU.add,
+                    )
+                else:
+                    nc.scalar.activation(
+                        out=z[:, j, :],
+                        in_=h[:, j, :],
+                        func=ACT.Identity,
+                        bias=shift[:, j : j + 1],
+                        scale=rstd[:, j : j + 1],
+                    )
 
         def leaky_store(g, z, o, j0, j1):
             zf = z[:, j0:j1, :].rearrange("p j f -> p (j f)")
@@ -230,12 +239,6 @@ def tile_fcd_pa_t_kernel(tc, input1, input2, W1, b1, out):
                 out=out_view[:, (g * GT + j0) * F : (g * GT + j1) * F], in_=o[:, j0 * F : j1 * F]
             )
 
-        def stage_norm(g):
-            z = work.tile([P, GT, F], F32, tag="z", bufs=3)
-            live[("z", g)] = z
-            for j in range(GT):
-                norm_tile(g, z, j)
-
         def stage_leaky(g):
             o = work.tile([P, GT * F], F32, tag="o", bufs=3)
             if g < NG - 1:
@@ -244,24 +247,28 @@ def tile_fcd_pa_t_kernel(tc, input1, input2, W1, b1, out):
                 for j in range(GT):
                     leaky_store(g, live[("z", g)], o, j, j + 1)
 
-        for i in range(NG + 5):
+        stage_transpose(0)
+        for i in range(NG + 6):
+            if on(i + 1):
+                stage_transpose(i + 1)
             if on(i):
-                stage_transpose(i)
-            elif on(i - 3):
-                stage_std(i - 3)
+                stage_regroup(i)
+            elif on(i - 4):
+                stage_rstd(i - 4)
             if on(i - 1):
-                stage_matmul(i - 1)
-            if on(i - 3):
-                stage_rstd(i - 3)
-            if on(i - 4):
-                stage_norm(i - 4)
-            if on(i - 5) and i - 5 < NG - 1:
+                stage_quantise(i - 1)
+            if on(i - 5):
+                stage_norm(i - 5)
+            if on(i - 6) and i - 6 < NG - 1:
+                stage_leaky(i - 6)
+            if i - 5 == NG - 1:
                 stage_leaky(i - 5)
-            if i - 4 == NG - 1:
-                stage_leaky(i - 4)
+            if on(i - 4):
+                stage_shift(i - 4)
             if on(i - 3):
-                stage_shift(i - 3)
-            if on(i - 2):
-                stage_squares(i - 2)
-            if on(i - 1):
-                stage_bias(i - 1)
+                stage_squares(i - 3)
+            for j in range(GT):
+                if on(i - 2):
+                    bias_tile(i - 2, j)
+                if on(i - 1):
+                    matmul_tile(i - 1, j)

@@ -14,26 +14,25 @@ ALU = mybir.AluOpType
 ACT = mybir.ActivationFunctionType
 
 P = 128
-ROWS = 8192
 HALF = 256
-K = 512
+K = 2 * HALF
 F = 512
-TILES = ROWS // P
-GT = 4
-NG = TILES // GT
+ROW_TILES = 8192 // P
+GROUP = 4
+GROUPS = ROW_TILES // GROUP
 EPS = 1e-5
 SLOPE = 0.2
-CHUNKS = [4, 4, 8, 8, 8, 8, 8, 8, 8]
-GPSIMD_NORM_TILES = 2
+LOAD_TILES = [4, 4, 4, 4, 8, 8, 8, 8, 8, 8]
+GPSIMD_TILES = 2
 
 
 def tile_fcd_pa_t_kernel(tc, input1, input2, W1, b1, out):
     nc = tc.nc
     x_views = (
-        input1.rearrange("(p t) o d -> p (t o d)", t=TILES),
-        input2.rearrange("(p t) o d -> p (t o d)", t=TILES),
+        input1.rearrange("(p t) o d -> p (t o d)", t=ROW_TILES),
+        input2.rearrange("(p t) o d -> p (t o d)", t=ROW_TILES),
     )
-    out_view = out.rearrange("(p t) o f -> p (t o f)", t=TILES)
+    out_view = out.rearrange("(p t) o f -> p (t o f)", t=ROW_TILES)
     w_view = W1.rearrange("(j p) k -> p j k", p=P)
 
     with ExitStack() as stack:
@@ -45,230 +44,223 @@ def tile_fcd_pa_t_kernel(tc, input1, input2, W1, b1, out):
 
         w_words = []
         for b in range(2):
-            wraw = const.tile([P, 2 * K], BF16, name="wraw%d" % b)
+            w_rows = const.tile([P, 2 * K], BF16, name="w_rows%d" % b)
             nc.sync.dma_start(
-                out=wraw[:].rearrange("p (j k) -> p j k", j=2), in_=w_view[:, 2 * b : 2 * b + 2, :]
+                out=w_rows[:].rearrange("p (j k) -> p j k", j=2), in_=w_view[:, 2 * b : 2 * b + 2, :]
             )
-            w_words.append(wraw[:].bitcast(F32))
-        braw = const.tile([P, F], BF16)
-        nc.scalar.dma_start(out=braw[:], in_=b1.partition_broadcast(P))
+            w_words.append(w_rows[:].bitcast(F32))
         x_words = {}
         first = 0
-        for c, n in enumerate(CHUNKS):
+        for c, n in enumerate(LOAD_TILES):
             views = []
             for s in range(2):
-                xin = const.tile([P, n * HALF], BF16, name="x%d_%d" % (s, c))
-                nc.sync.dma_start(out=xin[:], in_=x_views[s][:, first * HALF : (first + n) * HALF])
-                views.append(xin[:].bitcast(F32))
+                x_rows = const.tile([P, n * HALF], BF16, name="x_rows%d_%d" % (s, c))
+                nc.sync.dma_start(out=x_rows[:], in_=x_views[s][:, first * HALF : (first + n) * HALF])
+                views.append(x_rows[:].bitcast(F32))
             for t in range(n):
                 x_words[first + t] = (views[0], views[1], t)
             first += n
 
-        ident = const.tile([P, P], F32)
-        make_identity(nc, ident[:])
-        one = const.tile([P, 1], F32)
-        nc.vector.memset(one[:], 1.0)
+        bias_row = const.tile([P, F], BF16)
+        nc.vector.memset(bias_row[:], 0.0)
+        nc.scalar.dma_start(out=bias_row[0:1, :], in_=b1.rearrange("(o f) -> o f", o=1))
+        ones = const.tile([P, P], BF16)
+        nc.vector.memset(ones[:], 1.0)
+        identity = const.tile([P, P], F32)
+        make_identity(nc, identity[:])
+        unit = const.tile([P, 1], F32)
+        nc.vector.memset(unit[:], 1.0)
         warm = const.tile([P, 1], F32)
-        nc.scalar.activation(out=warm[:], in_=one[:], func=ACT.Abs_reciprocal_sqrt)
+        nc.scalar.activation(out=warm[:], in_=unit[:], func=ACT.Abs_reciprocal_sqrt)
 
-        def transpose_group(word_block):
+        def transpose_four(word_block):
             banks = []
             for b in range(2):
-                xt = psum.tile([P, 2, 2, P], F32, tag="xt")
-                for jj in range(2):
+                bank = psum.tile([P, 2, 2, P], F32, tag="words")
+                for j in range(2):
                     for u in range(2):
-                        nc.tensor.transpose(xt[:, jj, u, :], word_block(2 * b + jj, u), ident[:])
-                banks.append(xt)
+                        nc.tensor.transpose(bank[:, j, u, :], word_block(2 * b + j, u), identity[:])
+                banks.append(bank)
             return banks
 
-        def regroup(banks, grouped, b, on_vector):
-            gw = grouped[:].bitcast(F32).rearrange("p (j r u) -> p j r u", j=GT, u=2)
-            dst = gw[:, 2 * b : 2 * b + 2, :, :]
-            src = banks[b][:].rearrange("p j u r -> p j r u")
-            if on_vector:
-                nc.vector.tensor_copy(out=dst, in_=src)
-            else:
-                nc.scalar.copy(out=dst, in_=src)
+        def regroup(copy, bank, grouped, b):
+            words = grouped[:].bitcast(F32).rearrange("p (j r u) -> p j r u", j=GROUP, u=2)
+            copy(out=words[:, 2 * b : 2 * b + 2, :, :], in_=bank[:].rearrange("p j u r -> p j r u"))
 
         def w_block(j, u):
             start = (j % 2) * HALF + u * P
             return w_words[j // 2][:, start : start + P]
 
-        w_banks = transpose_group(w_block)
-        w_grouped = const.tile([P, GT * K], BF16, align_bytes=64)
-        regroup(w_banks, w_grouped, 0, True)
-        regroup(w_banks, w_grouped, 1, True)
+        w_banks = transpose_four(w_block)
+        w_grouped = const.tile([P, GROUP * K], BF16, align_bytes=64)
+        regroup(nc.vector.tensor_copy, w_banks[0], w_grouped, 0)
+        regroup(nc.vector.tensor_copy, w_banks[1], w_grouped, 1)
         w_codes = const.tile([P, F], U32, align_bytes=64)
         w_scales = const.tile([P, F], U8, align_bytes=64)
         nc.vector.quantize_mx(out=w_codes[:].bitcast(FP8X4), scales=w_scales[:], in_=w_grouped[:])
-        bias = const.tile([P, F], F32)
-        nc.vector.tensor_copy(out=bias[:], in_=braw[:])
 
-        live = {}
+        banks, grouped, codes, scales, product = {}, {}, {}, {}, {}
+        hidden, row_sum, square_sum, rstd, shift, normed = {}, {}, {}, {}, {}, {}
 
-        def on(g):
-            return 0 <= g < NG
-
-        def x_block(g):
-            def block(j, u):
-                entry = x_words[g * GT + j]
+        def transpose_x(g):
+            def x_block(j, u):
+                entry = x_words[g * GROUP + j]
                 return entry[u][:, entry[2] * P : (entry[2] + 1) * P]
 
-            return block
+            banks[g] = transpose_four(x_block)
 
-        def stage_transpose(g):
-            live[("banks", g)] = transpose_group(x_block(g))
+        def regroup_x(g, b):
+            if b == 0:
+                grouped_new = work.tile([P, GROUP * K], BF16, tag="grouped", align_bytes=64)
+                grouped[g] = grouped_new
+            regroup(nc.scalar.copy, banks[g][b], grouped[g], b)
 
-        def stage_regroup(g):
-            banks = live[("banks", g)]
-            grouped = work.tile([P, GT * K], BF16, tag="xg", align_bytes=64)
-            regroup(banks, grouped, 0, False)
-            if on(g - 4):
-                stage_rstd(g - 4)
-            regroup(banks, grouped, 1, False)
-            live[("grouped", g)] = grouped
-
-        def stage_quantise(g):
-            codes = work.tile([P, GT * P], U32, tag="xc", align_bytes=64)
-            scales = work.tile([P, GT * P], U8, tag="xs", align_bytes=64)
+        def quantise_x(g):
+            codes_new = work.tile([P, GROUP * P], U32, tag="codes", align_bytes=64)
+            scales_new = work.tile([P, GROUP * P], U8, tag="scales", align_bytes=64)
             nc.vector.quantize_mx(
-                out=codes[:].bitcast(FP8X4), scales=scales[:], in_=live[("grouped", g)][:]
+                out=codes_new[:].bitcast(FP8X4), scales=scales_new[:], in_=grouped[g][:]
             )
-            live[("q", g)] = (codes, scales)
+            codes[g] = codes_new
+            scales[g] = scales_new
 
-        def matmul_tile(g, j):
-            codes, scales = live[("q", g)]
-            y = psum.tile([P, F], F32, tag="y")
+        def multiply(g, j):
+            bank = psum.tile([P, F], F32, tag="product")
             nc.tensor.matmul_mx(
-                out=y[:],
-                lhsT=codes[:, j * P : (j + 1) * P].bitcast(FP8X4),
-                lhsT_scale=scales[:, j * P : (j + 1) * P],
+                out=bank[:],
+                lhsT=codes[g][:, j * P : (j + 1) * P].bitcast(FP8X4),
+                lhsT_scale=scales[g][:, j * P : (j + 1) * P],
                 rhs=w_codes[:].bitcast(FP8X4),
                 rhs_scale=w_scales[:],
                 start=True,
                 stop=True,
             )
-            live[("y", g, j)] = y
+            product[(g, j)] = bank
 
-        def bias_tile(g, j):
+        def add_bias(g, j):
             if j == 0:
-                h_new = work.tile([P, GT, F], F32, tag="h", bufs=5)
-                sums_new = stats.tile([P, GT], F32, tag="sums")
-                live[("h", g)] = h_new
-                live[("sums", g)] = sums_new
+                hidden_new = work.tile([P, GROUP, F], F32, tag="hidden", bufs=5)
+                row_sum_new = stats.tile([P, GROUP], F32, tag="row_sum")
+                hidden[g] = hidden_new
+                row_sum[g] = row_sum_new
             nc.vector.scalar_tensor_tensor(
-                out=live[("h", g)][:, j, :],
-                in0=live[("y", g, j)][:],
+                out=hidden[g][:, j, :],
+                in0=product[(g, j)][:],
                 scalar=1.0,
                 in1=bias[:],
                 op0=ALU.mult,
                 op1=ALU.add,
-                accum_out=live[("sums", g)][:, j : j + 1],
+                accum_out=row_sum[g][:, j : j + 1],
             )
 
-        def stage_squares(g):
-            h = live[("h", g)]
-            sums = live[("sums", g)]
-            ssq = stats.tile([P, GT], F32, tag="ssq")
-            for j in range(GT):
-                junk = work.tile([P, F], BF16, tag="junk")
+        def sum_squares(g):
+            square_sum_new = stats.tile([P, GROUP], F32, tag="square_sum")
+            square_sum[g] = square_sum_new
+            for j in range(GROUP):
+                squares = work.tile([P, F], BF16, tag="squares")
                 nc.scalar.activation(
-                    out=junk[:],
-                    in_=h[:, j, :],
+                    out=squares[:],
+                    in_=hidden[g][:, j, :],
                     func=ACT.Square,
-                    bias=sums[:, j : j + 1],
+                    bias=row_sum[g][:, j : j + 1],
                     scale=-1.0 * F,
-                    accum_out=ssq[:, j : j + 1],
+                    accum_out=square_sum[g][:, j : j + 1],
                 )
-            live[("ssq", g)] = ssq
 
-        def stage_rstd(g):
-            rstd = stats.tile([P, GT], F32, tag="rstd")
+        def reciprocal_std(g):
+            rstd_new = stats.tile([P, GROUP], F32, tag="rstd")
             nc.scalar.activation(
-                out=rstd[:],
-                in_=live[("ssq", g)][:],
+                out=rstd_new[:],
+                in_=square_sum[g][:],
                 func=ACT.Abs_reciprocal_sqrt,
                 bias=EPS,
                 scale=1.0 / (F * F * F),
             )
-            live[("rstd", g)] = rstd
+            rstd[g] = rstd_new
 
-        def stage_shift(g):
-            shift = stats.tile([P, GT], F32, tag="shift")
+        def mean_shift(g):
+            shift_new = stats.tile([P, GROUP], F32, tag="shift")
             nc.vector.scalar_tensor_tensor(
-                out=shift[:],
-                in0=live[("sums", g)][:],
+                out=shift_new[:],
+                in0=row_sum[g][:],
                 scalar=-1.0 / F,
-                in1=live[("rstd", g)][:],
+                in1=rstd[g][:],
                 op0=ALU.mult,
                 op1=ALU.mult,
             )
-            live[("shift", g)] = shift
+            shift[g] = shift_new
 
-        def stage_norm(g):
-            h = live[("h", g)]
-            rstd = live[("rstd", g)]
-            shift = live[("shift", g)]
-            z = work.tile([P, GT, F], F32, tag="z", bufs=3)
-            live[("z", g)] = z
-            for j in range(GT):
-                if j < GPSIMD_NORM_TILES and g < NG - 1:
+        def normalise(g):
+            normed_new = work.tile([P, GROUP, F], F32, tag="normed", bufs=3)
+            normed[g] = normed_new
+            for j in range(GROUP):
+                if j < GPSIMD_TILES and g < GROUPS - 2:
                     nc.gpsimd.tensor_scalar(
-                        out=z[:, j, :],
-                        in0=h[:, j, :],
-                        scalar1=rstd[:, j : j + 1],
-                        scalar2=shift[:, j : j + 1],
+                        out=normed[g][:, j, :],
+                        in0=hidden[g][:, j, :],
+                        scalar1=rstd[g][:, j : j + 1],
+                        scalar2=shift[g][:, j : j + 1],
                         op0=ALU.mult,
                         op1=ALU.add,
                     )
                 else:
                     nc.scalar.activation(
-                        out=z[:, j, :],
-                        in_=h[:, j, :],
+                        out=normed[g][:, j, :],
+                        in_=hidden[g][:, j, :],
                         func=ACT.Identity,
-                        bias=shift[:, j : j + 1],
-                        scale=rstd[:, j : j + 1],
+                        bias=shift[g][:, j : j + 1],
+                        scale=rstd[g][:, j : j + 1],
                     )
 
-        def leaky_store(g, z, o, j0, j1):
-            zf = z[:, j0:j1, :].rearrange("p j f -> p (j f)")
-            nc.vector.scalar_tensor_tensor(
-                out=o[:, j0 * F : j1 * F], in0=zf, scalar=SLOPE, in1=zf, op0=ALU.mult, op1=ALU.max
-            )
-            nc.sync.dma_start(
-                out=out_view[:, (g * GT + j0) * F : (g * GT + j1) * F], in_=o[:, j0 * F : j1 * F]
-            )
+        def leaky_and_store(g, pieces):
+            result = work.tile([P, GROUP * F], F32, tag="result", bufs=3)
+            width = GROUP * F // pieces
+            flat = normed[g][:].rearrange("p j f -> p (j f)")
+            for c in range(pieces):
+                cols = slice(c * width, (c + 1) * width)
+                nc.vector.scalar_tensor_tensor(
+                    out=result[:, cols],
+                    in0=flat[:, cols],
+                    scalar=SLOPE,
+                    in1=flat[:, cols],
+                    op0=ALU.mult,
+                    op1=ALU.max,
+                )
+                nc.sync.dma_start(
+                    out=out_view[:, g * GROUP * F + c * width : g * GROUP * F + (c + 1) * width],
+                    in_=result[:, cols],
+                )
 
-        def stage_leaky(g):
-            o = work.tile([P, GT * F], F32, tag="o", bufs=3)
-            if g < NG - 1:
-                leaky_store(g, live[("z", g)], o, 0, GT)
-            else:
-                for j in range(GT):
-                    leaky_store(g, live[("z", g)], o, j, j + 1)
+        transpose_x(0)
+        bias_bank = psum.tile([P, F], F32, tag="product")
+        nc.tensor.matmul(out=bias_bank[:], lhsT=ones[:], rhs=bias_row[:], start=True, stop=True)
+        bias = const.tile([P, F], F32)
+        nc.vector.tensor_copy(out=bias[:], in_=bias_bank[:])
 
-        stage_transpose(0)
-        for i in range(NG + 6):
-            if on(i + 1):
-                stage_transpose(i + 1)
-            if on(i):
-                stage_regroup(i)
-            elif on(i - 4):
-                stage_rstd(i - 4)
-            if on(i - 1):
-                stage_quantise(i - 1)
-            if on(i - 5):
-                stage_norm(i - 5)
-            if on(i - 6) and i - 6 < NG - 1:
-                stage_leaky(i - 6)
-            if i - 5 == NG - 1:
-                stage_leaky(i - 5)
-            if on(i - 4):
-                stage_shift(i - 4)
-            if on(i - 3):
-                stage_squares(i - 3)
-            for j in range(GT):
-                if on(i - 2):
-                    bias_tile(i - 2, j)
-                if on(i - 1):
-                    matmul_tile(i - 1, j)
+        def live(g):
+            return 0 <= g < GROUPS
+
+        for i in range(GROUPS + 6):
+            if live(i + 1):
+                transpose_x(i + 1)
+            if live(i):
+                regroup_x(i, 0)
+            if live(i - 4):
+                reciprocal_std(i - 4)
+            if live(i):
+                regroup_x(i, 1)
+            if live(i - 1):
+                quantise_x(i - 1)
+            if live(i - 5):
+                normalise(i - 5)
+            if live(i - 6):
+                leaky_and_store(i - 6, GROUP if i - 6 == GROUPS - 1 else 1)
+            if live(i - 4):
+                mean_shift(i - 4)
+            if live(i - 3):
+                sum_squares(i - 3)
+            for j in range(GROUP):
+                if live(i - 2):
+                    add_bias(i - 2, j)
+                if live(i - 1):
+                    multiply(i - 1, j)

@@ -241,7 +241,7 @@ def tile_fcd_pa_t_kernel(tc, input1, input2, W1, b1, out):
             return 0 <= g < GROUPS
 
         for i in range(GROUPS + 6):
-            if live(i + 1):
+            if live(i + 1) and i != 1:
                 transpose_x(i + 1)
             if live(i):
                 regroup_x(i, 0)
@@ -264,3 +264,5 @@ def tile_fcd_pa_t_kernel(tc, input1, input2, W1, b1, out):
                     add_bias(i - 2, j)
                 if live(i - 1):
                     multiply(i - 1, j)
+            if i == 1:
+                transpose_x(i + 1)

from contextlib import ExitStack

import concourse.mybir as mybir
from concourse.masks import make_identity

FLOPS = 2 * 8192 * 512 * 512

F32 = mybir.dt.float32
BF16 = mybir.dt.bfloat16
U32 = mybir.dt.uint32
U8 = mybir.dt.uint8
FP8X4 = mybir.dt.float8_e4m3fn_x4
ALU = mybir.AluOpType
ACT = mybir.ActivationFunctionType

P = 128
HALF = 256
K = 2 * HALF
F = 512
ROW_TILES = 8192 // P
GROUP = 4
GROUPS = ROW_TILES // GROUP
EPS = 1e-5
SLOPE = 0.2
LOAD_TILES = [4, 4, 4, 4, 8, 8, 8, 8, 8, 8]
GPSIMD_TILES = 2


def tile_fcd_pa_t_kernel(tc, input1, input2, W1, b1, out):
    nc = tc.nc
    x_views = (
        input1.rearrange("(p t) o d -> p (t o d)", t=ROW_TILES),
        input2.rearrange("(p t) o d -> p (t o d)", t=ROW_TILES),
    )
    out_view = out.rearrange("(p t) o f -> p (t o f)", t=ROW_TILES)
    w_view = W1.rearrange("(j p) k -> p j k", p=P)

    with ExitStack() as stack:
        const = stack.enter_context(tc.tile_pool(name="const", bufs=1))
        work = stack.enter_context(tc.tile_pool(name="work", bufs=2))
        stats = stack.enter_context(tc.tile_pool(name="stats", bufs=8))
        psum = stack.enter_context(tc.psum_pool(name="psum", bufs=4))
        stack.enter_context(tc.manual_schedule())

        w_words = []
        for b in range(2):
            w_rows = const.tile([P, 2 * K], BF16, name="w_rows%d" % b)
            nc.sync.dma_start(
                out=w_rows[:].rearrange("p (j k) -> p j k", j=2), in_=w_view[:, 2 * b : 2 * b + 2, :]
            )
            w_words.append(w_rows[:].bitcast(F32))
        x_words = {}
        first = 0
        for c, n in enumerate(LOAD_TILES):
            views = []
            for s in range(2):
                x_rows = const.tile([P, n * HALF], BF16, name="x_rows%d_%d" % (s, c))
                nc.sync.dma_start(out=x_rows[:], in_=x_views[s][:, first * HALF : (first + n) * HALF])
                views.append(x_rows[:].bitcast(F32))
            for t in range(n):
                x_words[first + t] = (views[0], views[1], t)
            first += n

        bias_row = const.tile([P, F], BF16)
        nc.vector.memset(bias_row[:], 0.0)
        nc.scalar.dma_start(out=bias_row[0:1, :], in_=b1.rearrange("(o f) -> o f", o=1))
        ones = const.tile([P, P], BF16)
        nc.vector.memset(ones[:], 1.0)
        identity = const.tile([P, P], F32)
        make_identity(nc, identity[:])
        unit = const.tile([P, 1], F32)
        nc.vector.memset(unit[:], 1.0)
        warm = const.tile([P, 1], F32)
        nc.scalar.activation(out=warm[:], in_=unit[:], func=ACT.Abs_reciprocal_sqrt)

        def transpose_four(word_block):
            banks = []
            for b in range(2):
                bank = psum.tile([P, 2, 2, P], F32, tag="words")
                for j in range(2):
                    for u in range(2):
                        nc.tensor.transpose(bank[:, j, u, :], word_block(2 * b + j, u), identity[:])
                banks.append(bank)
            return banks

        def regroup(copy, bank, grouped, b):
            words = grouped[:].bitcast(F32).rearrange("p (j r u) -> p j r u", j=GROUP, u=2)
            copy(out=words[:, 2 * b : 2 * b + 2, :, :], in_=bank[:].rearrange("p j u r -> p j r u"))

        def w_block(j, u):
            start = (j % 2) * HALF + u * P
            return w_words[j // 2][:, start : start + P]

        w_banks = transpose_four(w_block)
        w_grouped = const.tile([P, GROUP * K], BF16, align_bytes=64)
        regroup(nc.vector.tensor_copy, w_banks[0], w_grouped, 0)
        regroup(nc.vector.tensor_copy, w_banks[1], w_grouped, 1)
        w_codes = const.tile([P, F], U32, align_bytes=64)
        w_scales = const.tile([P, F], U8, align_bytes=64)
        nc.vector.quantize_mx(out=w_codes[:].bitcast(FP8X4), scales=w_scales[:], in_=w_grouped[:])

        banks, grouped, codes, scales, product = {}, {}, {}, {}, {}
        hidden, row_sum, square_sum, rstd, shift, normed = {}, {}, {}, {}, {}, {}

        def transpose_x(g):
            def x_block(j, u):
                entry = x_words[g * GROUP + j]
                return entry[u][:, entry[2] * P : (entry[2] + 1) * P]

            banks[g] = transpose_four(x_block)

        def regroup_x(g, b):
            if b == 0:
                grouped_new = work.tile([P, GROUP * K], BF16, tag="grouped", align_bytes=64)
                grouped[g] = grouped_new
            regroup(nc.scalar.copy, banks[g][b], grouped[g], b)

        def quantise_x(g):
            codes_new = work.tile([P, GROUP * P], U32, tag="codes", align_bytes=64)
            scales_new = work.tile([P, GROUP * P], U8, tag="scales", align_bytes=64)
            nc.vector.quantize_mx(
                out=codes_new[:].bitcast(FP8X4), scales=scales_new[:], in_=grouped[g][:]
            )
            codes[g] = codes_new
            scales[g] = scales_new

        def multiply(g, j):
            bank = psum.tile([P, F], F32, tag="product")
            nc.tensor.matmul_mx(
                out=bank[:],
                lhsT=codes[g][:, j * P : (j + 1) * P].bitcast(FP8X4),
                lhsT_scale=scales[g][:, j * P : (j + 1) * P],
                rhs=w_codes[:].bitcast(FP8X4),
                rhs_scale=w_scales[:],
                start=True,
                stop=True,
            )
            product[(g, j)] = bank

        def add_bias(g, j):
            if j == 0:
                hidden_new = work.tile([P, GROUP, F], F32, tag="hidden", bufs=5)
                row_sum_new = stats.tile([P, GROUP], F32, tag="row_sum")
                hidden[g] = hidden_new
                row_sum[g] = row_sum_new
            nc.vector.scalar_tensor_tensor(
                out=hidden[g][:, j, :],
                in0=product[(g, j)][:],
                scalar=1.0,
                in1=bias[:],
                op0=ALU.mult,
                op1=ALU.add,
                accum_out=row_sum[g][:, j : j + 1],
            )

        def sum_squares(g):
            square_sum_new = stats.tile([P, GROUP], F32, tag="square_sum")
            square_sum[g] = square_sum_new
            for j in range(GROUP):
                squares = work.tile([P, F], BF16, tag="squares")
                nc.scalar.activation(
                    out=squares[:],
                    in_=hidden[g][:, j, :],
                    func=ACT.Square,
                    bias=row_sum[g][:, j : j + 1],
                    scale=-1.0 * F,
                    accum_out=square_sum[g][:, j : j + 1],
                )

        def reciprocal_std(g):
            rstd_new = stats.tile([P, GROUP], F32, tag="rstd")
            nc.scalar.activation(
                out=rstd_new[:],
                in_=square_sum[g][:],
                func=ACT.Abs_reciprocal_sqrt,
                bias=EPS,
                scale=1.0 / (F * F * F),
            )
            rstd[g] = rstd_new

        def mean_shift(g):
            shift_new = stats.tile([P, GROUP], F32, tag="shift")
            nc.vector.scalar_tensor_tensor(
                out=shift_new[:],
                in0=row_sum[g][:],
                scalar=-1.0 / F,
                in1=rstd[g][:],
                op0=ALU.mult,
                op1=ALU.mult,
            )
            shift[g] = shift_new

        def normalise(g):
            normed_new = work.tile([P, GROUP, F], F32, tag="normed", bufs=3)
            normed[g] = normed_new
            for j in range(GROUP):
                if j < GPSIMD_TILES and g < GROUPS - 2:
                    nc.gpsimd.tensor_scalar(
                        out=normed[g][:, j, :],
                        in0=hidden[g][:, j, :],
                        scalar1=rstd[g][:, j : j + 1],
                        scalar2=shift[g][:, j : j + 1],
                        op0=ALU.mult,
                        op1=ALU.add,
                    )
                else:
                    nc.scalar.activation(
                        out=normed[g][:, j, :],
                        in_=hidden[g][:, j, :],
                        func=ACT.Identity,
                        bias=shift[g][:, j : j + 1],
                        scale=rstd[g][:, j : j + 1],
                    )

        def leaky_and_store(g, pieces):
            result = work.tile([P, GROUP * F], F32, tag="result", bufs=3)
            width = GROUP * F // pieces
            flat = normed[g][:].rearrange("p j f -> p (j f)")
            for c in range(pieces):
                cols = slice(c * width, (c + 1) * width)
                nc.vector.scalar_tensor_tensor(
                    out=result[:, cols],
                    in0=flat[:, cols],
                    scalar=SLOPE,
                    in1=flat[:, cols],
                    op0=ALU.mult,
                    op1=ALU.max,
                )
                nc.sync.dma_start(
                    out=out_view[:, g * GROUP * F + c * width : g * GROUP * F + (c + 1) * width],
                    in_=result[:, cols],
                )

        transpose_x(0)
        bias_bank = psum.tile([P, F], F32, tag="product")
        nc.tensor.matmul(out=bias_bank[:], lhsT=ones[:], rhs=bias_row[:], start=True, stop=True)
        bias = const.tile([P, F], F32)
        nc.vector.tensor_copy(out=bias[:], in_=bias_bank[:])

        def live(g):
            return 0 <= g < GROUPS

        for i in range(GROUPS + 6):
            if live(i + 1) and i != 1:
                transpose_x(i + 1)
            if live(i):
                regroup_x(i, 0)
            if live(i - 4):
                reciprocal_std(i - 4)
            if live(i):
                regroup_x(i, 1)
            if live(i - 1):
                quantise_x(i - 1)
            if live(i - 5):
                normalise(i - 5)
            if live(i - 6):
                leaky_and_store(i - 6, GROUP if i - 6 == GROUPS - 1 else 1)
            if live(i - 4):
                mean_shift(i - 4)
            if live(i - 3):
                sum_squares(i - 3)
            for j in range(GROUP):
                if live(i - 2):
                    add_bias(i - 2, j)
                if live(i - 1):
                    multiply(i - 1, j)
            if i == 1:
                transpose_x(i + 1)
